import numpy as np
import ml_dtypes


def mxq(x, axis, fmt="e4m3"):
    dtype, down = {"e4m3": (ml_dtypes.float8_e4m3fn, 7), "e5m2": (ml_dtypes.float8_e5m2, 14)}[fmt]
    v = np.moveaxis(np.asarray(x, np.float32).astype(ml_dtypes.bfloat16).astype(np.float64), axis, -1)
    blocks = v.reshape(v.shape[:-1] + (-1, 32))
    amax = np.abs(blocks).max(-1, keepdims=True)
    byte = np.maximum(np.where(amax > 0, np.frexp(amax)[1] - 1 + 127, 0) - down, 1)
    scale = np.exp2(byte - 127.0)
    codes = (blocks / scale).astype(np.float32).astype(dtype).astype(np.float64)
    return np.moveaxis((codes * scale).reshape(v.shape), -1, axis)


WIDE = False


def mx_kscale(k):
    if not WIDE:
        return np.ones(k)
    levels = np.array([10, -10, 5, -5, 0])
    a = np.random.permutation(np.resize(levels, k // 512 * 4)).reshape(k // 512, 4)
    idx = np.arange(k)
    return np.exp2(a[idx // 512, idx % 128 // 32])


BF16 = ml_dtypes.bfloat16


def bf(x):
    return np.asarray(x, np.float32).astype(BF16)


def f64(x):
    return np.asarray(x).astype(np.float64)


B, S, D, H, DH, DV, R = 2, 64, 512, 16, 64, 64, 512
EPS = 1e-6
ROPE_THETA = 10000.0


def rms_norm(c, w):
    var = np.mean(np.square(c), axis=-1, keepdims=True)
    return c * (1.0 / np.sqrt(var + EPS)) * w


def apply_rope(t, cos, sin):
    b, s, h, d = t.shape
    tr = t.reshape(b, s, h, d // 2, 2)
    x1, x2 = tr[..., 0], tr[..., 1]
    c = cos[None, :, None, :]
    sn = sin[None, :, None, :]
    o1 = x1 * c - x2 * sn
    o2 = x1 * sn + x2 * c
    return np.stack([o1, o2], axis=-1).reshape(b, s, h, d)


def setup_inputs():
    s = mx_kscale(D)
    t = mx_kscale(R)
    inv_freq = 1.0 / ROPE_THETA ** (np.arange(0, DH, 2) / DH)
    ang = np.arange(S)[:, None] * inv_freq[None, :]
    return {"x": bf(np.random.standard_normal((B, S, D)) * s),
            "freqs_cos": bf(np.cos(ang)),
            "freqs_sin": bf(np.sin(ang)),
            "w_kv_compress": bf(np.random.standard_normal((D, R)) / np.sqrt(D) / s[:, None]),
            "kv_norm_w": bf((1.0 + 0.1 * np.random.standard_normal(R)) * t),
            "w_k_up": bf(np.random.standard_normal((R, H * DH)) / np.sqrt(R) / t[:, None]),
            "w_v_up": bf(np.random.standard_normal((R, H * DV)) / np.sqrt(R) / t[:, None])}


def reference(x, freqs_cos, freqs_sin, w_kv_compress, kv_norm_w, w_k_up, w_v_up):
    c = mxq(f64(x), 2, "e4m3") @ mxq(f64(w_kv_compress), 0, "e4m3")
    latent_q = mxq(rms_norm(c, f64(kv_norm_w)), 2, "e4m3")
    k = (latent_q @ mxq(f64(w_k_up), 0, "e4m3")).reshape(B, S, H, DH)
    v = (latent_q @ mxq(f64(w_v_up), 0, "e4m3")).reshape(B, S, H, DV)
    return apply_rope(k, f64(freqs_cos), f64(freqs_sin)), v

@@ -1,0 +1,225 @@
+from contextlib import ExitStack
+
+import concourse.mybir as mybir
+from concourse.masks import make_identity
+
+F32 = mybir.dt.float32
+BF16 = mybir.dt.bfloat16
+U32 = mybir.dt.uint32
+U8 = mybir.dt.uint8
+FP8X4 = mybir.dt.float8_e4m3fn_x4
+ACT = mybir.ActivationFunctionType
+ALU = mybir.AluOpType
+
+P = 128
+PACK = 4
+BATCH = 2
+SEQ = 64
+D_MODEL = 512
+RANK = 512
+HEADS = 16
+HEAD_DIM = 64
+PAIRS = HEAD_DIM // 2
+CHUNK = 512
+CHUNK_HEADS = CHUNK // HEAD_DIM
+CHUNK_PAIRS = CHUNK // 2
+RUN = 4
+EPS = 1e-6
+
+VECTOR_COLS_C = 336
+VECTOR_COLS_K = 256
+VECTOR_COLS_V = 0
+
+FLOPS = 2 * P * D_MODEL * RANK + 2 * 2 * P * RANK * HEADS * HEAD_DIM
+
+
+def tile_mla_pa_s_kernel(
+    tc, x, freqs_cos, freqs_sin, w_kv_compress, kv_norm_w, w_k_up, w_v_up, out_0, out_1
+):
+    nc = tc.nc
+    x_rows = x.rearrange("b s d -> (b s) d")
+    out_rows = {
+        "k": out_0.rearrange("b s h d -> (b s) (h d)"),
+        "v": out_1.rearrange("b s h d -> (b s) (h d)"),
+    }
+
+    with ExitStack() as ctx:
+        keep = ctx.enter_context(tc.tile_pool(name="keep", bufs=1))
+        psum = ctx.enter_context(tc.psum_pool(name="psum", bufs=1))
+        ctx.enter_context(tc.manual_schedule())
+
+        raw = {}
+        grouped = {}
+        words = {}
+        scales = {}
+
+        def load_chunk(name, weight, first_col):
+            raw[name] = keep.tile([P, PACK, CHUNK], BF16, name="raw_%s" % name)
+            grouped[name] = keep.tile(
+                [P, CHUNK, PACK], BF16, name="grouped_%s" % name, align_bytes=64
+            )
+            words[name] = keep.tile([P, CHUNK], U32, name="words_%s" % name, align_bytes=64)
+            scales[name] = keep.tile([P, CHUNK], U8, name="scales_%s" % name, align_bytes=64)
+            rows = weight.rearrange("(p t) c -> p t c", t=PACK)
+            nc.sync.dma_start(out=raw[name][:], in_=rows[:, :, first_col : first_col + CHUNK])
+
+        def regroup(copy, name, cols):
+            copy(
+                out=grouped[name][:, cols, :].rearrange("p (c i) t -> p c t i", i=RUN),
+                in_=raw[name][:, :, cols].rearrange("p t (c i) -> p c t i", i=RUN),
+            )
+
+        def regroup_chunk(name, vector_cols):
+            if vector_cols > 0:
+                regroup(nc.vector.tensor_copy, name, slice(0, vector_cols))
+            regroup(nc.scalar.copy, name, slice(vector_cols, CHUNK))
+
+        def quantise_chunk(name):
+            nc.vector.quantize_mx(
+                out=words[name][:].bitcast(FP8X4),
+                scales=scales[name][:],
+                in_=grouped[name][:].rearrange("p c t -> p (c t)"),
+            )
+
+        def multiply(name, rows_q, rows_s):
+            acc = psum.tile([P, CHUNK], F32, name="acc_%s" % name)
+            nc.tensor.matmul_mx(
+                out=acc[:],
+                lhsT=rows_q[:].bitcast(FP8X4),
+                lhsT_scale=rows_s[:],
+                rhs=words[name][:].bitcast(FP8X4),
+                rhs_scale=scales[name][:],
+                start=True,
+                stop=True,
+            )
+            return acc
+
+        x_sb = keep.tile([P, D_MODEL], BF16)
+        nc.sync.dma_start(out=x_sb[:], in_=x_rows)
+        load_chunk("c", w_kv_compress, 0)
+        load_chunk("k0", w_k_up, 0)
+        load_chunk("k1", w_k_up, CHUNK)
+        load_chunk("v0", w_v_up, 0)
+        load_chunk("v1", w_v_up, CHUNK)
+        gain = keep.tile([P, PACK], BF16)
+        nc.scalar.dma_start(out=gain[:], in_=kv_norm_w.rearrange("(p t) -> p t", t=PACK))
+        cos_sb = keep.tile([P, PAIRS], BF16)
+        sin_sb = keep.tile([P, PAIRS], BF16)
+        for b in range(BATCH):
+            nc.scalar.dma_start(out=cos_sb[b * SEQ : (b + 1) * SEQ, :], in_=freqs_cos)
+            nc.scalar.dma_start(out=sin_sb[b * SEQ : (b + 1) * SEQ, :], in_=freqs_sin)
+
+        ident = keep.tile([P, P], F32)
+        make_identity(nc, ident[:])
+        one = keep.tile([P, 1], F32)
+        nc.vector.memset(one[:], 1.0)
+        warm = keep.tile([P, 1], F32)
+        nc.scalar.activation(out=warm[:], in_=one[:], func=ACT.Sqrt)
+
+        x_words = x_sb[:].bitcast(F32).rearrange("r (p u) -> r u p", u=2)
+        xT_ps = psum.tile([P, 2, P], F32)
+        for u in range(2):
+            nc.tensor.transpose(xT_ps[:, u, :], x_words[:, u, :], ident[:])
+        x_grouped = keep.tile([P, P * PACK], BF16, align_bytes=64)
+        nc.scalar.copy(
+            out=x_grouped[:].bitcast(F32).rearrange("p (r u) -> p r u", u=2),
+            in_=xT_ps[:].rearrange("p u r -> p r u"),
+        )
+        x_q = keep.tile([P, P], U32, align_bytes=64)
+        x_s = keep.tile([P, P], U8, align_bytes=64)
+        nc.vector.quantize_mx(out=x_q[:].bitcast(FP8X4), scales=x_s[:], in_=x_grouped[:])
+
+        regroup_chunk("c", VECTOR_COLS_C)
+        quantise_chunk("c")
+        c_ps = multiply("c", x_q, x_s)
+
+        regroup_chunk("k0", VECTOR_COLS_K)
+        squares = keep.tile([P, RANK], BF16)
+        sum_sq = keep.tile([P, 1], F32)
+        nc.scalar.activation(out=squares[:], in_=c_ps[:], func=ACT.Square, accum_out=sum_sq[:])
+        rms = keep.tile([P, 1], F32)
+        nc.scalar.activation(out=rms[:], in_=sum_sq[:], func=ACT.Sqrt, scale=1.0 / RANK, bias=EPS)
+        quantise_chunk("k0")
+        rstd = keep.tile([P, 1], F32)
+        nc.vector.reciprocal(out=rstd[:], in_=rms[:])
+        c_norm = keep.tile([P, PACK, P], F32)
+        nc.vector.tensor_scalar(
+            out=c_norm[:],
+            in0=c_ps[:].rearrange("r (p t) -> r t p", t=PACK),
+            scalar1=rstd[:],
+            scalar2=None,
+            op0=ALU.mult,
+        )
+        normT_ps = psum.tile([P, PACK, P], F32)
+        for t in range(PACK):
+            nc.tensor.transpose(normT_ps[:, t, :], c_norm[:, t, :], ident[:])
+        regroup_chunk("k1", VECTOR_COLS_K)
+        latent = keep.tile([P, P, PACK], BF16, align_bytes=64)
+        nc.vector.tensor_tensor(
+            out=latent[:],
+            in0=normT_ps[:].rearrange("p t r -> p r t"),
+            in1=gain[:].unsqueeze(1).to_broadcast([P, P, PACK]),
+            op=ALU.mult,
+        )
+        latent_q = keep.tile([P, P], U32, align_bytes=64)
+        latent_s = keep.tile([P, P], U8, align_bytes=64)
+        nc.vector.quantize_mx(
+            out=latent_q[:].bitcast(FP8X4),
+            scales=latent_s[:],
+            in_=latent[:].rearrange("p r t -> p (r t)"),
+        )
+        quantise_chunk("k1")
+
+        rot = {}
+        cross = {}
+
+        def rotation_products(h, k_ps):
+            pairs = "r (h i e) -> r h i e"
+            halves = k_ps[:].rearrange("r (h i e) -> r e h i", i=PAIRS, e=2)
+            sin_bc = sin_sb[:].unsqueeze(1).to_broadcast([P, CHUNK_HEADS, PAIRS])
+            rot[h] = keep.tile([P, CHUNK], F32, name="rot_%d" % h)
+            cross[h] = keep.tile([P, 2, CHUNK_PAIRS], F32, name="cross_%d" % h)
+            nc.vector.tensor_tensor(
+                out=rot[h][:].rearrange(pairs, i=PAIRS, e=2),
+                in0=k_ps[:].rearrange(pairs, i=PAIRS, e=2),
+                in1=cos_sb[:].unsqueeze(1).unsqueeze(3).to_broadcast([P, CHUNK_HEADS, PAIRS, 2]),
+                op=ALU.mult,
+            )
+            nc.vector.scalar_tensor_tensor(
+                out=cross[h][:, 0, :].rearrange("r (h i) -> r h i", i=PAIRS),
+                in0=halves[:, 1],
+                scalar=-1.0,
+                in1=sin_bc,
+                op0=ALU.mult,
+                op1=ALU.mult,
+            )
+            nc.vector.tensor_tensor(
+                out=cross[h][:, 1, :].rearrange("r (h i) -> r h i", i=PAIRS),
+                in0=halves[:, 0],
+                in1=sin_bc,
+                op=ALU.mult,
+            )
+
+        def rotation_sum(h):
+            nc.vector.tensor_tensor(
+                out=rot[h][:].rearrange("r (c e) -> r c e", e=2),
+                in0=rot[h][:].rearrange("r (c e) -> r c e", e=2),
+                in1=cross[h][:].rearrange("r e c -> r c e"),
+                op=ALU.add,
+            )
+            nc.sync.dma_start(out=out_rows["k"][:, h * CHUNK : (h + 1) * CHUNK], in_=rot[h][:])
+
+        k_ps = [multiply("k%d" % h, latent_q, latent_s) for h in range(2)]
+        regroup_chunk("v0", VECTOR_COLS_V)
+        regroup_chunk("v1", VECTOR_COLS_V)
+        v_ps = []
+        for h in range(2):
+            rotation_products(h, k_ps[h])
+            quantise_chunk("v%d" % h)
+            v_ps.append(multiply("v%d" % h, latent_q, latent_s))
+        for h in range(2):
+            rotation_sum(h)
+        for h in range(2):
+            v_sb = keep.tile([P, CHUNK], F32, name="v_sb_%d" % h)
+            nc.scalar.copy(out=v_sb[:], in_=v_ps[h][:])
+            nc.scalar.dma_start(out=out_rows["v"][:, h * CHUNK : (h + 1) * CHUNK], in_=v_sb[:])

@@ -22,13 +22,11 @@ HEAD_DIM = 64
 PAIRS = HEAD_DIM // 2
 CHUNK = 512
 CHUNK_HEADS = CHUNK // HEAD_DIM
-CHUNK_PAIRS = CHUNK // 2
+C_CHUNK = RANK // 2
 RUN = 4
 EPS = 1e-6
 
-VECTOR_COLS_C = 336
-VECTOR_COLS_K = 256
-VECTOR_COLS_V = 0
+VECTOR_COLS = {"c0": 168, "c1": 168, "k0": 256, "k1": 192, "v0": 64, "v1": 256}
 
 FLOPS = 2 * P * D_MODEL * RANK + 2 * 2 * P * RANK * HEADS * HEAD_DIM
 
@@ -38,10 +36,8 @@ def tile_mla_pa_s_kernel(
 ):
     nc = tc.nc
     x_rows = x.rearrange("b s d -> (b s) d")
-    out_rows = {
-        "k": out_0.rearrange("b s h d -> (b s) (h d)"),
-        "v": out_1.rearrange("b s h d -> (b s) (h d)"),
-    }
+    k_rows = out_0.rearrange("b s h d -> (b s) (h d)")
+    v_rows = out_1.rearrange("b s h d -> (b s) (h d)")
 
     with ExitStack() as ctx:
         keep = ctx.enter_context(tc.tile_pool(name="keep", bufs=1))
@@ -53,15 +49,14 @@ def tile_mla_pa_s_kernel(
         words = {}
         scales = {}
 
-        def load_chunk(name, weight, first_col):
-            raw[name] = keep.tile([P, PACK, CHUNK], BF16, name="raw_%s" % name)
+        def load_chunk(name, rows, first_col, width):
+            raw[name] = keep.tile([P, PACK, width], BF16, name="raw_%s" % name)
             grouped[name] = keep.tile(
-                [P, CHUNK, PACK], BF16, name="grouped_%s" % name, align_bytes=64
+                [P, width, PACK], BF16, name="grouped_%s" % name, align_bytes=64
             )
-            words[name] = keep.tile([P, CHUNK], U32, name="words_%s" % name, align_bytes=64)
-            scales[name] = keep.tile([P, CHUNK], U8, name="scales_%s" % name, align_bytes=64)
-            rows = weight.rearrange("(p t) c -> p t c", t=PACK)
-            nc.sync.dma_start(out=raw[name][:], in_=rows[:, :, first_col : first_col + CHUNK])
+            words[name] = keep.tile([P, width], U32, name="words_%s" % name, align_bytes=64)
+            scales[name] = keep.tile([P, width], U8, name="scales_%s" % name, align_bytes=64)
+            nc.sync.dma_start(out=raw[name][:], in_=rows[:, :, first_col : first_col + width])
 
         def regroup(copy, name, cols):
             copy(
@@ -69,10 +64,11 @@ def tile_mla_pa_s_kernel(
                 in_=raw[name][:, :, cols].rearrange("p t (c i) -> p c t i", i=RUN),
             )
 
-        def regroup_chunk(name, vector_cols):
-            if vector_cols > 0:
-                regroup(nc.vector.tensor_copy, name, slice(0, vector_cols))
-            regroup(nc.scalar.copy, name, slice(vector_cols, CHUNK))
+        def regroup_vector(name):
+            regroup(nc.vector.tensor_copy, name, slice(0, VECTOR_COLS[name]))
+
+        def regroup_scalar(name):
+            regroup(nc.scalar.copy, name, slice(VECTOR_COLS[name], raw[name].shape[2]))
 
         def quantise_chunk(name):
             nc.vector.quantize_mx(
@@ -81,45 +77,57 @@ def tile_mla_pa_s_kernel(
                 in_=grouped[name][:].rearrange("p c t -> p (c t)"),
             )
 
-        def multiply(name, rows_q, rows_s):
-            acc = psum.tile([P, CHUNK], F32, name="acc_%s" % name)
+        def matmul(out, lhsT, rhs):
             nc.tensor.matmul_mx(
-                out=acc[:],
-                lhsT=rows_q[:].bitcast(FP8X4),
-                lhsT_scale=rows_s[:],
-                rhs=words[name][:].bitcast(FP8X4),
-                rhs_scale=scales[name][:],
+                out=out,
+                lhsT=lhsT[0].bitcast(FP8X4),
+                lhsT_scale=lhsT[1],
+                rhs=rhs[0].bitcast(FP8X4),
+                rhs_scale=rhs[1],
                 start=True,
                 stop=True,
             )
-            return acc
 
         x_sb = keep.tile([P, D_MODEL], BF16)
         nc.sync.dma_start(out=x_sb[:], in_=x_rows)
-        load_chunk("c", w_kv_compress, 0)
-        load_chunk("k0", w_k_up, 0)
-        load_chunk("k1", w_k_up, CHUNK)
-        load_chunk("v0", w_v_up, 0)
-        load_chunk("v1", w_v_up, CHUNK)
-        gain = keep.tile([P, PACK], BF16)
-        nc.scalar.dma_start(out=gain[:], in_=kv_norm_w.rearrange("(p t) -> p t", t=PACK))
-        cos_sb = keep.tile([P, PAIRS], BF16)
-        sin_sb = keep.tile([P, PAIRS], BF16)
-        for b in range(BATCH):
-            nc.scalar.dma_start(out=cos_sb[b * SEQ : (b + 1) * SEQ, :], in_=freqs_cos)
-            nc.scalar.dma_start(out=sin_sb[b * SEQ : (b + 1) * SEQ, :], in_=freqs_sin)
+        gain_rows = keep.tile([P, P], BF16)
+        nc.vector.memset(gain_rows[:], 0.0)
+        nc.sync.dma_start(
+            out=gain_rows[0:PACK, :], in_=kv_norm_w.rearrange("(t p) -> t p", t=PACK)
+        )
+        c_view = w_kv_compress.rearrange("(p t) c -> p t c", t=PACK)
+        k_view = w_k_up.rearrange("(t p) c -> p t c", t=PACK)
+        v_view = w_v_up.rearrange("(t p) c -> p t c", t=PACK)
+        for h in range(2):
+            load_chunk("c%d" % h, c_view, h * C_CHUNK, C_CHUNK)
+        for h in range(2):
+            load_chunk("k%d" % h, k_view, h * CHUNK, CHUNK)
+        for h in range(2):
+            load_chunk("v%d" % h, v_view, h * CHUNK, CHUNK)
 
         ident = keep.tile([P, P], F32)
         make_identity(nc, ident[:])
         one = keep.tile([P, 1], F32)
         nc.vector.memset(one[:], 1.0)
         warm = keep.tile([P, 1], F32)
-        nc.scalar.activation(out=warm[:], in_=one[:], func=ACT.Sqrt)
+        nc.scalar.activation(out=warm[:], in_=one[:], func=ACT.Abs_reciprocal_sqrt)
+        cos_sb = keep.tile([P, PAIRS], BF16)
+        sin_sb = keep.tile([P, PAIRS], BF16)
+        for b in range(BATCH):
+            nc.gpsimd.dma_start(out=cos_sb[b * SEQ : (b + 1) * SEQ, :], in_=freqs_cos)
+            nc.gpsimd.dma_start(out=sin_sb[b * SEQ : (b + 1) * SEQ, :], in_=freqs_sin)
+        unit = keep.tile([P, PACK], BF16)
+        nc.vector.tensor_copy(out=unit[:], in_=ident[:, 0:PACK])
 
         x_words = x_sb[:].bitcast(F32).rearrange("r (p u) -> r u p", u=2)
-        xT_ps = psum.tile([P, 2, P], F32)
+        xT_ps = psum.tile([P, 2, P], F32, name="bank_x")
         for u in range(2):
             nc.tensor.transpose(xT_ps[:, u, :], x_words[:, u, :], ident[:])
+        gain_ps = psum.tile([P, PACK], F32, name="bank_gain")
+        nc.tensor.matmul(gain_ps[:], lhsT=gain_rows[:], rhs=unit[:], start=True, stop=True)
+        gain = keep.tile([P, PACK], F32)
+        nc.vector.tensor_copy(out=gain[:], in_=gain_ps[:])
+
         x_grouped = keep.tile([P, P * PACK], BF16, align_bytes=64)
         nc.scalar.copy(
             out=x_grouped[:].bitcast(F32).rearrange("p (r u) -> p r u", u=2),
@@ -127,40 +135,73 @@ def tile_mla_pa_s_kernel(
         )
         x_q = keep.tile([P, P], U32, align_bytes=64)
         x_s = keep.tile([P, P], U8, align_bytes=64)
+        x_mx = (x_q[:], x_s[:])
+
+        c_tok = []
+        c_chan = []
+
+        def multiply_c(h):
+            name = "c%d" % h
+            c_tok.append(psum.tile([P, C_CHUNK], F32, name="bank_tok%d" % h))
+            matmul(c_tok[h][:], x_mx, (words[name][:], scales[name][:]))
+            c_chan.append(psum.tile([P, 2, P], F32, name="bank_chan%d" % h))
+            for u in range(2):
+                cols = slice(u * P, (u + 1) * P)
+                matmul(c_chan[h][:, u, :], (words[name][:, cols], scales[name][:, cols]), x_mx)
+
+        regroup_vector("c0")
+        regroup_scalar("c0")
         nc.vector.quantize_mx(out=x_q[:].bitcast(FP8X4), scales=x_s[:], in_=x_grouped[:])
+        quantise_chunk("c0")
+        multiply_c(0)
+        regroup_vector("c1")
+        regroup_scalar("c1")
+        quantise_chunk("c1")
+        multiply_c(1)
 
-        regroup_chunk("c", VECTOR_COLS_C)
-        quantise_chunk("c")
-        c_ps = multiply("c", x_q, x_s)
+        sums = []
+        for h in range(2):
+            squares = keep.tile([P, C_CHUNK], BF16, name="squares%d" % h)
+            sums.append(keep.tile([P, 1], F32, name="sum%d" % h))
+            nc.scalar.activation(
+                out=squares[:], in_=c_tok[h][:], func=ACT.Square, accum_out=sums[h][:]
+            )
+        c_gain = keep.tile([P, PACK, P], F32)
 
-        regroup_chunk("k0", VECTOR_COLS_K)
-        squares = keep.tile([P, RANK], BF16)
-        sum_sq = keep.tile([P, 1], F32)
-        nc.scalar.activation(out=squares[:], in_=c_ps[:], func=ACT.Square, accum_out=sum_sq[:])
-        rms = keep.tile([P, 1], F32)
-        nc.scalar.activation(out=rms[:], in_=sum_sq[:], func=ACT.Sqrt, scale=1.0 / RANK, bias=EPS)
-        quantise_chunk("k0")
-        rstd = keep.tile([P, 1], F32)
-        nc.vector.reciprocal(out=rstd[:], in_=rms[:])
-        c_norm = keep.tile([P, PACK, P], F32)
+        def apply_gain(h):
+            nc.vector.tensor_tensor(
+                out=c_gain[:, 2 * h : 2 * h + 2, :],
+                in0=c_chan[h][:],
+                in1=gain[:, 2 * h : 2 * h + 2].unsqueeze(2).to_broadcast([P, 2, P]),
+                op=ALU.mult,
+            )
+
+        apply_gain(0)
+        part = keep.tile([P, 1], F32)
         nc.vector.tensor_scalar(
-            out=c_norm[:],
-            in0=c_ps[:].rearrange("r (p t) -> r t p", t=PACK),
-            scalar1=rstd[:],
-            scalar2=None,
-            op0=ALU.mult,
+            out=part[:], in0=sums[0][:], scalar1=1.0 / RANK, scalar2=EPS, op0=ALU.mult, op1=ALU.add
         )
-        normT_ps = psum.tile([P, PACK, P], F32)
-        for t in range(PACK):
-            nc.tensor.transpose(normT_ps[:, t, :], c_norm[:, t, :], ident[:])
-        regroup_chunk("k1", VECTOR_COLS_K)
+        apply_gain(1)
+        rstd = keep.tile([P, 1], F32)
+        nc.scalar.activation(
+            out=rstd[:],
+            in_=sums[1][:],
+            func=ACT.Abs_reciprocal_sqrt,
+            scale=1.0 / RANK,
+            bias=part[:],
+        )
+        rstd_ps = psum.tile([P, P], F32, name="bank_gain")
+        nc.tensor.transpose(rstd_ps[:], rstd[:].to_broadcast([P, P]), ident[:])
+        regroup_vector("k0")
+        regroup_scalar("k0")
         latent = keep.tile([P, P, PACK], BF16, align_bytes=64)
         nc.vector.tensor_tensor(
             out=latent[:],
-            in0=normT_ps[:].rearrange("p t r -> p r t"),
-            in1=gain[:].unsqueeze(1).to_broadcast([P, P, PACK]),
+            in0=c_gain[:].rearrange("p t r -> p r t"),
+            in1=rstd_ps[:].unsqueeze(2).to_broadcast([P, P, PACK]),
             op=ALU.mult,
         )
+        quantise_chunk("k0")
         latent_q = keep.tile([P, P], U32, align_bytes=64)
         latent_s = keep.tile([P, P], U8, align_bytes=64)
         nc.vector.quantize_mx(
@@ -168,58 +209,70 @@ def tile_mla_pa_s_kernel(
             scales=latent_s[:],
             in_=latent[:].rearrange("p r t -> p (r t)"),
         )
-        quantise_chunk("k1")
+        latent_mx = (latent_q[:], latent_s[:])
 
+        def multiply_chunk(name, bank):
+            acc = psum.tile([P, CHUNK], F32, name=bank)
+            matmul(acc[:], latent_mx, (words[name][:], scales[name][:]))
+            return acc
+
+        signed_sin = keep.tile([P, PAIRS, 2], F32)
+        for e in range(2):
+            nc.gpsimd.tensor_scalar(
+                out=signed_sin[:, :, e],
+                in0=sin_sb[:],
+                scalar1=2.0 * e - 1.0,
+                scalar2=0.0,
+                op0=ALU.mult,
+                op1=ALU.add,
+            )
         rot = {}
         cross = {}
+        pairs = "r (h i e) -> r h i e"
 
         def rotation_products(h, k_ps):
-            pairs = "r (h i e) -> r h i e"
-            halves = k_ps[:].rearrange("r (h i e) -> r e h i", i=PAIRS, e=2)
-            sin_bc = sin_sb[:].unsqueeze(1).to_broadcast([P, CHUNK_HEADS, PAIRS])
-            rot[h] = keep.tile([P, CHUNK], F32, name="rot_%d" % h)
-            cross[h] = keep.tile([P, 2, CHUNK_PAIRS], F32, name="cross_%d" % h)
+            k_pairs = k_ps[:].rearrange(pairs, i=PAIRS, e=2)
+            rot[h] = keep.tile([P, CHUNK], F32, name="rot%d" % h)
+            cross[h] = keep.tile([P, CHUNK], F32, name="cross%d" % h)
+            shape = [P, CHUNK_HEADS, PAIRS, 2]
             nc.vector.tensor_tensor(
                 out=rot[h][:].rearrange(pairs, i=PAIRS, e=2),
-                in0=k_ps[:].rearrange(pairs, i=PAIRS, e=2),
-                in1=cos_sb[:].unsqueeze(1).unsqueeze(3).to_broadcast([P, CHUNK_HEADS, PAIRS, 2]),
+                in0=k_pairs,
+                in1=cos_sb[:].unsqueeze(1).unsqueeze(3).to_broadcast(shape),
                 op=ALU.mult,
             )
-            nc.vector.scalar_tensor_tensor(
-                out=cross[h][:, 0, :].rearrange("r (h i) -> r h i", i=PAIRS),
-                in0=halves[:, 1],
-                scalar=-1.0,
-                in1=sin_bc,
-                op0=ALU.mult,
-                op1=ALU.mult,
-            )
             nc.vector.tensor_tensor(
-                out=cross[h][:, 1, :].rearrange("r (h i) -> r h i", i=PAIRS),
-                in0=halves[:, 0],
-                in1=sin_bc,
+                out=cross[h][:].rearrange(pairs, i=PAIRS, e=2),
+                in0=k_pairs[:, :, :, ::-1],
+                in1=signed_sin[:].unsqueeze(1).to_broadcast(shape),
                 op=ALU.mult,
             )
 
-        def rotation_sum(h):
-            nc.vector.tensor_tensor(
-                out=rot[h][:].rearrange("r (c e) -> r c e", e=2),
-                in0=rot[h][:].rearrange("r (c e) -> r c e", e=2),
-                in1=cross[h][:].rearrange("r e c -> r c e"),
-                op=ALU.add,
-            )
-            nc.sync.dma_start(out=out_rows["k"][:, h * CHUNK : (h + 1) * CHUNK], in_=rot[h][:])
+        def rotation_sum(engine, h):
+            engine.tensor_tensor(out=rot[h][:], in0=rot[h][:], in1=cross[h][:], op=ALU.add)
+            nc.sync.dma_start(out=k_rows[:, h * CHUNK : (h + 1) * CHUNK], in_=rot[h][:])
 
-        k_ps = [multiply("k%d" % h, latent_q, latent_s) for h in range(2)]
-        regroup_chunk("v0", VECTOR_COLS_V)
-        regroup_chunk("v1", VECTOR_COLS_V)
-        v_ps = []
-        for h in range(2):
-            rotation_products(h, k_ps[h])
-            quantise_chunk("v%d" % h)
-            v_ps.append(multiply("v%d" % h, latent_q, latent_s))
-        for h in range(2):
-            rotation_sum(h)
-        for h in range(2):
-            v_sb = keep.tile([P, CHUNK], F32, name="v_sb_%d" % h)
-            nc.scalar.copy(out=v_sb[:], in_=v_ps[h][:])
-            nc.scalar.dma_start(out=out_rows["v"][:, h * CHUNK : (h + 1) * CHUNK], in_=v_sb[:])
+        def store_v(h, acc):
+            v_sb = keep.tile([P, CHUNK], F32, name="v_sb%d" % h)
+            nc.scalar.copy(out=v_sb[:], in_=acc[:])
+            nc.scalar.dma_start(out=v_rows[:, h * CHUNK : (h + 1) * CHUNK], in_=v_sb[:])
+
+        k0_ps = multiply_chunk("k0", "bank_k0")
+        regroup_vector("k1")
+        regroup_scalar("k1")
+        rotation_products(0, k0_ps)
+        rotation_sum(nc.gpsimd, 0)
+        quantise_chunk("k1")
+        k1_ps = multiply_chunk("k1", "bank_k1")
+        regroup_scalar("v0")
+        regroup_vector("v0")
+        regroup_scalar("v1")
+        regroup_vector("v1")
+        quantise_chunk("v0")
+        v0_ps = multiply_chunk("v0", "bank_tok0")
+        rotation_products(1, k1_ps)
+        store_v(0, v0_ps)
+        quantise_chunk("v1")
+        v1_ps = multiply_chunk("v1", "bank_tok1")
+        rotation_sum(nc.vector, 1)
+        store_v(1, v1_ps)

@@ -26,7 +26,7 @@ C_CHUNK = RANK // 2
 RUN = 4
 EPS = 1e-6
 
-VECTOR_COLS = {"c0": 168, "c1": 168, "k0": 256, "k1": 192, "v0": 64, "v1": 256}
+VECTOR_COLS = {"c0": 200, "c1": 128, "k0": 512, "k1": 0, "v0": 0, "v1": 304}
 
 FLOPS = 2 * P * D_MODEL * RANK + 2 * 2 * P * RANK * HEADS * HEAD_DIM
 
@@ -65,10 +65,13 @@ def tile_mla_pa_s_kernel(
             )
 
         def regroup_vector(name):
-            regroup(nc.vector.tensor_copy, name, slice(0, VECTOR_COLS[name]))
+            if VECTOR_COLS[name] > 0:
+                regroup(nc.vector.tensor_copy, name, slice(0, VECTOR_COLS[name]))
 
         def regroup_scalar(name):
-            regroup(nc.scalar.copy, name, slice(VECTOR_COLS[name], raw[name].shape[2]))
+            width = raw[name].shape[2]
+            if VECTOR_COLS[name] < width:
+                regroup(nc.scalar.copy, name, slice(VECTOR_COLS[name], width))
 
         def quantise_chunk(name):
             nc.vector.quantize_mx(
@@ -100,8 +103,13 @@ def tile_mla_pa_s_kernel(
         v_view = w_v_up.rearrange("(t p) c -> p t c", t=PACK)
         for h in range(2):
             load_chunk("c%d" % h, c_view, h * C_CHUNK, C_CHUNK)
-        for h in range(2):
-            load_chunk("k%d" % h, k_view, h * CHUNK, CHUNK)
+        load_chunk("k0", k_view, 0, CHUNK)
+        cos_sb = keep.tile([P, PAIRS], BF16)
+        sin_sb = keep.tile([P, PAIRS], BF16)
+        for b in range(BATCH):
+            nc.sync.dma_start(out=cos_sb[b * SEQ : (b + 1) * SEQ, :], in_=freqs_cos)
+            nc.sync.dma_start(out=sin_sb[b * SEQ : (b + 1) * SEQ, :], in_=freqs_sin)
+        load_chunk("k1", k_view, CHUNK, CHUNK)
         for h in range(2):
             load_chunk("v%d" % h, v_view, h * CHUNK, CHUNK)
 
@@ -111,11 +119,6 @@ def tile_mla_pa_s_kernel(
         nc.vector.memset(one[:], 1.0)
         warm = keep.tile([P, 1], F32)
         nc.scalar.activation(out=warm[:], in_=one[:], func=ACT.Abs_reciprocal_sqrt)
-        cos_sb = keep.tile([P, PAIRS], BF16)
-        sin_sb = keep.tile([P, PAIRS], BF16)
-        for b in range(BATCH):
-            nc.gpsimd.dma_start(out=cos_sb[b * SEQ : (b + 1) * SEQ, :], in_=freqs_cos)
-            nc.gpsimd.dma_start(out=sin_sb[b * SEQ : (b + 1) * SEQ, :], in_=freqs_sin)
         unit = keep.tile([P, PACK], BF16)
         nc.vector.tensor_copy(out=unit[:], in_=ident[:, 0:PACK])
 
@@ -160,12 +163,17 @@ def tile_mla_pa_s_kernel(
         multiply_c(1)
 
         sums = []
-        for h in range(2):
+
+        def sum_squares(h):
             squares = keep.tile([P, C_CHUNK], BF16, name="squares%d" % h)
             sums.append(keep.tile([P, 1], F32, name="sum%d" % h))
             nc.scalar.activation(
                 out=squares[:], in_=c_tok[h][:], func=ACT.Square, accum_out=sums[h][:]
             )
+
+        sum_squares(0)
+        sum_squares(1)
+        regroup_vector("k0")
         c_gain = keep.tile([P, PACK, P], F32)
 
         def apply_gain(h):
@@ -182,6 +190,7 @@ def tile_mla_pa_s_kernel(
             out=part[:], in0=sums[0][:], scalar1=1.0 / RANK, scalar2=EPS, op0=ALU.mult, op1=ALU.add
         )
         apply_gain(1)
+        quantise_chunk("k0")
         rstd = keep.tile([P, 1], F32)
         nc.scalar.activation(
             out=rstd[:],
@@ -192,8 +201,9 @@ def tile_mla_pa_s_kernel(
         )
         rstd_ps = psum.tile([P, P], F32, name="bank_gain")
         nc.tensor.transpose(rstd_ps[:], rstd[:].to_broadcast([P, P]), ident[:])
-        regroup_vector("k0")
         regroup_scalar("k0")
+        regroup_vector("k1")
+        regroup_scalar("k1")
         latent = keep.tile([P, P, PACK], BF16, align_bytes=64)
         nc.vector.tensor_tensor(
             out=latent[:],
@@ -201,7 +211,6 @@ def tile_mla_pa_s_kernel(
             in1=rstd_ps[:].unsqueeze(2).to_broadcast([P, P, PACK]),
             op=ALU.mult,
         )
-        quantise_chunk("k0")
         latent_q = keep.tile([P, P], U32, align_bytes=64)
         latent_s = keep.tile([P, P], U8, align_bytes=64)
         nc.vector.quantize_mx(
@@ -248,9 +257,13 @@ def tile_mla_pa_s_kernel(
                 op=ALU.mult,
             )
 
-        def rotation_sum(engine, h):
-            engine.tensor_tensor(out=rot[h][:], in0=rot[h][:], in1=cross[h][:], op=ALU.add)
-            nc.sync.dma_start(out=k_rows[:, h * CHUNK : (h + 1) * CHUNK], in_=rot[h][:])
+        def rotation_sum(engine, h, first, width):
+            cols = slice(first, first + width)
+            engine.tensor_tensor(
+                out=rot[h][:, cols], in0=rot[h][:, cols], in1=cross[h][:, cols], op=ALU.add
+            )
+            out_cols = slice(h * CHUNK + first, h * CHUNK + first + width)
+            nc.sync.dma_start(out=k_rows[:, out_cols], in_=rot[h][:, cols])
 
         def store_v(h, acc):
             v_sb = keep.tile([P, CHUNK], F32, name="v_sb%d" % h)
@@ -258,21 +271,19 @@ def tile_mla_pa_s_kernel(
             nc.scalar.dma_start(out=v_rows[:, h * CHUNK : (h + 1) * CHUNK], in_=v_sb[:])
 
         k0_ps = multiply_chunk("k0", "bank_k0")
-        regroup_vector("k1")
-        regroup_scalar("k1")
-        rotation_products(0, k0_ps)
-        rotation_sum(nc.gpsimd, 0)
         quantise_chunk("k1")
         k1_ps = multiply_chunk("k1", "bank_k1")
         regroup_scalar("v0")
-        regroup_vector("v0")
         regroup_scalar("v1")
+        rotation_products(0, k0_ps)
+        rotation_sum(nc.gpsimd, 0, 0, CHUNK)
         regroup_vector("v1")
         quantise_chunk("v0")
         v0_ps = multiply_chunk("v0", "bank_tok0")
-        rotation_products(1, k1_ps)
-        store_v(0, v0_ps)
         quantise_chunk("v1")
         v1_ps = multiply_chunk("v1", "bank_tok1")
-        rotation_sum(nc.vector, 1)
+        store_v(0, v0_ps)
         store_v(1, v1_ps)
+        rotation_products(1, k1_ps)
+        rotation_sum(nc.vector, 1, 0, CHUNK // 2)
+        rotation_sum(nc.vector, 1, CHUNK // 2, CHUNK // 2)

@@ -26,7 +26,7 @@ C_CHUNK = RANK // 2
 RUN = 4
 EPS = 1e-6
 
-VECTOR_COLS = {"c0": 200, "c1": 128, "k0": 512, "k1": 0, "v0": 0, "v1": 304}
+VECTOR_COLS = {"c0": 200, "c1": 128, "k0": 512, "k1": 184, "v0": 96, "v1": 96}
 
 FLOPS = 2 * P * D_MODEL * RANK + 2 * 2 * P * RANK * HEADS * HEAD_DIM
 
@@ -171,25 +171,26 @@ def tile_mla_pa_s_kernel(
                 out=squares[:], in_=c_tok[h][:], func=ACT.Square, accum_out=sums[h][:]
             )
 
-        sum_squares(0)
-        sum_squares(1)
-        regroup_vector("k0")
         c_gain = keep.tile([P, PACK, P], F32)
 
         def apply_gain(h):
-            nc.vector.tensor_tensor(
-                out=c_gain[:, 2 * h : 2 * h + 2, :],
-                in0=c_chan[h][:],
-                in1=gain[:, 2 * h : 2 * h + 2].unsqueeze(2).to_broadcast([P, 2, P]),
-                op=ALU.mult,
-            )
+            for u in range(2):
+                t = 2 * h + u
+                nc.scalar.activation(
+                    out=c_gain[:, t, :],
+                    in_=c_chan[h][:, u, :],
+                    func=ACT.Copy,
+                    scale=gain[:, t : t + 1],
+                )
 
-        apply_gain(0)
+        sum_squares(0)
         part = keep.tile([P, 1], F32)
-        nc.vector.tensor_scalar(
+        nc.gpsimd.tensor_scalar(
             out=part[:], in0=sums[0][:], scalar1=1.0 / RANK, scalar2=EPS, op0=ALU.mult, op1=ALU.add
         )
-        apply_gain(1)
+        apply_gain(0)
+        sum_squares(1)
+        regroup_vector("k0")
         quantise_chunk("k0")
         rstd = keep.tile([P, 1], F32)
         nc.scalar.activation(
@@ -201,6 +202,7 @@ def tile_mla_pa_s_kernel(
         )
         rstd_ps = psum.tile([P, P], F32, name="bank_gain")
         nc.tensor.transpose(rstd_ps[:], rstd[:].to_broadcast([P, P]), ident[:])
+        apply_gain(1)
         regroup_scalar("k0")
         regroup_vector("k1")
         regroup_scalar("k1")
@@ -268,13 +270,14 @@ def tile_mla_pa_s_kernel(
         def store_v(h, acc):
             v_sb = keep.tile([P, CHUNK], F32, name="v_sb%d" % h)
             nc.scalar.copy(out=v_sb[:], in_=acc[:])
-            nc.scalar.dma_start(out=v_rows[:, h * CHUNK : (h + 1) * CHUNK], in_=v_sb[:])
+            nc.sync.dma_start(out=v_rows[:, h * CHUNK : (h + 1) * CHUNK], in_=v_sb[:])
 
         k0_ps = multiply_chunk("k0", "bank_k0")
         quantise_chunk("k1")
         k1_ps = multiply_chunk("k1", "bank_k1")
         regroup_scalar("v0")
         regroup_scalar("v1")
+        regroup_vector("v0")
         rotation_products(0, k0_ps)
         rotation_sum(nc.gpsimd, 0, 0, CHUNK)
         regroup_vector("v1")

@@ -26,7 +26,9 @@ C_CHUNK = RANK // 2
 RUN = 4
 EPS = 1e-6
 
-VECTOR_COLS = {"c0": 200, "c1": 128, "k0": 512, "k1": 184, "v0": 96, "v1": 96}
+VECTOR_COLS = {"c0": 200, "c1": 128, "k0": 512, "k1": 184, "v0": 96, "v1": 160}
+GPSIMD_COLS = {"v0": 128, "v1": 192}
+GPSIMD_PIECES = 2
 
 FLOPS = 2 * P * D_MODEL * RANK + 2 * 2 * P * RANK * HEADS * HEAD_DIM
 
@@ -68,10 +70,22 @@ def tile_mla_pa_s_kernel(
             if VECTOR_COLS[name] > 0:
                 regroup(nc.vector.tensor_copy, name, slice(0, VECTOR_COLS[name]))
 
+        def copy_gpsimd(out, in_):
+            nc.gpsimd.tensor_scalar(
+                out=out, in0=in_, scalar1=1.0, scalar2=0.0, op0=ALU.mult, op1=ALU.add
+            )
+
+        def regroup_gpsimd(name):
+            piece = GPSIMD_COLS[name] // GPSIMD_PIECES
+            for i in range(GPSIMD_PIECES):
+                first = VECTOR_COLS[name] + i * piece
+                regroup(copy_gpsimd, name, slice(first, first + piece))
+
         def regroup_scalar(name):
             width = raw[name].shape[2]
-            if VECTOR_COLS[name] < width:
-                regroup(nc.scalar.copy, name, slice(VECTOR_COLS[name], width))
+            first = VECTOR_COLS[name] + GPSIMD_COLS.get(name, 0)
+            if first < width:
+                regroup(nc.scalar.copy, name, slice(first, width))
 
         def quantise_chunk(name):
             nc.vector.quantize_mx(
@@ -237,6 +251,8 @@ def tile_mla_pa_s_kernel(
                 op0=ALU.mult,
                 op1=ALU.add,
             )
+        regroup_gpsimd("v0")
+        regroup_gpsimd("v1")
         rot = {}
         cross = {}
         pairs = "r (h i e) -> r h i e"

@@ -26,7 +26,7 @@ C_CHUNK = RANK // 2
 RUN = 4
 EPS = 1e-6
 
-VECTOR_COLS = {"c0": 200, "c1": 128, "k0": 512, "k1": 184, "v0": 96, "v1": 160}
+VECTOR_COLS = {"c0": 256, "c1": 96, "k0": 512, "k1": 184, "v0": 96, "v1": 160}
 GPSIMD_COLS = {"v0": 128, "v1": 192}
 GPSIMD_PIECES = 2
 
@@ -107,16 +107,16 @@ def tile_mla_pa_s_kernel(
 
         x_sb = keep.tile([P, D_MODEL], BF16)
         nc.sync.dma_start(out=x_sb[:], in_=x_rows)
-        gain_rows = keep.tile([P, P], BF16)
-        nc.vector.memset(gain_rows[:], 0.0)
-        nc.sync.dma_start(
-            out=gain_rows[0:PACK, :], in_=kv_norm_w.rearrange("(t p) -> t p", t=PACK)
-        )
         c_view = w_kv_compress.rearrange("(p t) c -> p t c", t=PACK)
         k_view = w_k_up.rearrange("(t p) c -> p t c", t=PACK)
         v_view = w_v_up.rearrange("(t p) c -> p t c", t=PACK)
         for h in range(2):
             load_chunk("c%d" % h, c_view, h * C_CHUNK, C_CHUNK)
+        gain_rows = keep.tile([P, P], BF16)
+        nc.vector.memset(gain_rows[:], 0.0)
+        nc.sync.dma_start(
+            out=gain_rows[0:PACK, :], in_=kv_norm_w.rearrange("(t p) -> t p", t=PACK)
+        )
         load_chunk("k0", k_view, 0, CHUNK)
         cos_sb = keep.tile([P, PAIRS], BF16)
         sin_sb = keep.tile([P, PAIRS], BF16)
@@ -143,8 +143,6 @@ def tile_mla_pa_s_kernel(
         gain_ps = psum.tile([P, PACK], F32, name="bank_gain")
         nc.tensor.matmul(gain_ps[:], lhsT=gain_rows[:], rhs=unit[:], start=True, stop=True)
         gain = keep.tile([P, PACK], F32)
-        nc.vector.tensor_copy(out=gain[:], in_=gain_ps[:])
-
         x_grouped = keep.tile([P, P * PACK], BF16, align_bytes=64)
         nc.scalar.copy(
             out=x_grouped[:].bitcast(F32).rearrange("p (r u) -> p r u", u=2),
@@ -170,6 +168,7 @@ def tile_mla_pa_s_kernel(
         regroup_scalar("c0")
         nc.vector.quantize_mx(out=x_q[:].bitcast(FP8X4), scales=x_s[:], in_=x_grouped[:])
         quantise_chunk("c0")
+        nc.vector.tensor_copy(out=gain[:], in_=gain_ps[:])
         multiply_c(0)
         regroup_vector("c1")
         regroup_scalar("c1")

@@ -51,14 +51,20 @@ def tile_mla_pa_s_kernel(
         words = {}
         scales = {}
 
-        def load_chunk(name, rows, first_col, width):
-            raw[name] = keep.tile([P, PACK, width], BF16, name="raw_%s" % name)
+        def load(names, view, first_col, width):
+            cols = len(names) * width
+            tile = keep.tile([P, PACK, cols], BF16, name="raw_%s" % names[0])
+            nc.sync.dma_start(out=tile[:], in_=view[:, :, first_col : first_col + cols])
+            for i, name in enumerate(names):
+                make_chunk(name, tile[:, :, i * width : (i + 1) * width], width)
+
+        def make_chunk(name, raw_cols, width):
+            raw[name] = raw_cols
             grouped[name] = keep.tile(
                 [P, width, PACK], BF16, name="grouped_%s" % name, align_bytes=64
             )
             words[name] = keep.tile([P, width], U32, name="words_%s" % name, align_bytes=64)
             scales[name] = keep.tile([P, width], U8, name="scales_%s" % name, align_bytes=64)
-            nc.sync.dma_start(out=raw[name][:], in_=rows[:, :, first_col : first_col + width])
 
         def regroup(copy, name, cols):
             copy(
@@ -110,22 +116,21 @@ def tile_mla_pa_s_kernel(
         c_view = w_kv_compress.rearrange("(p t) c -> p t c", t=PACK)
         k_view = w_k_up.rearrange("(t p) c -> p t c", t=PACK)
         v_view = w_v_up.rearrange("(t p) c -> p t c", t=PACK)
-        for h in range(2):
-            load_chunk("c%d" % h, c_view, h * C_CHUNK, C_CHUNK)
+        load(["c0", "c1"], c_view, 0, C_CHUNK)
         gain_rows = keep.tile([P, P], BF16)
         nc.vector.memset(gain_rows[:], 0.0)
         nc.sync.dma_start(
             out=gain_rows[0:PACK, :], in_=kv_norm_w.rearrange("(t p) -> t p", t=PACK)
         )
-        load_chunk("k0", k_view, 0, CHUNK)
+        load(["k0"], k_view, 0, CHUNK)
         cos_sb = keep.tile([P, PAIRS], BF16)
         sin_sb = keep.tile([P, PAIRS], BF16)
         for b in range(BATCH):
             nc.sync.dma_start(out=cos_sb[b * SEQ : (b + 1) * SEQ, :], in_=freqs_cos)
             nc.sync.dma_start(out=sin_sb[b * SEQ : (b + 1) * SEQ, :], in_=freqs_sin)
-        load_chunk("k1", k_view, CHUNK, CHUNK)
+        load(["k1"], k_view, CHUNK, CHUNK)
         for h in range(2):
-            load_chunk("v%d" % h, v_view, h * CHUNK, CHUNK)
+            load(["v%d" % h], v_view, h * CHUNK, CHUNK)
 
         ident = keep.tile([P, P], F32)
         make_identity(nc, ident[:])

@@ -26,7 +26,7 @@ C_CHUNK = RANK // 2
 RUN = 4
 EPS = 1e-6
 
-VECTOR_COLS = {"c0": 256, "c1": 96, "k0": 512, "k1": 184, "v0": 96, "v1": 160}
+VECTOR_COLS = {"c0": 256, "c1": 64, "k0": 512, "k1": 256, "v0": 64, "v1": 0}
 GPSIMD_COLS = {"v0": 128, "v1": 192}
 GPSIMD_PIECES = 2
 
@@ -149,7 +149,7 @@ def tile_mla_pa_s_kernel(
         nc.tensor.matmul(gain_ps[:], lhsT=gain_rows[:], rhs=unit[:], start=True, stop=True)
         gain = keep.tile([P, PACK], F32)
         x_grouped = keep.tile([P, P * PACK], BF16, align_bytes=64)
-        nc.scalar.copy(
+        nc.vector.tensor_copy(
             out=x_grouped[:].bitcast(F32).rearrange("p (r u) -> p r u", u=2),
             in_=xT_ps[:].rearrange("p u r -> p r u"),
         )
@@ -170,13 +170,12 @@ def tile_mla_pa_s_kernel(
                 matmul(c_chan[h][:, u, :], (words[name][:, cols], scales[name][:, cols]), x_mx)
 
         regroup_vector("c0")
-        regroup_scalar("c0")
-        nc.vector.quantize_mx(out=x_q[:].bitcast(FP8X4), scales=x_s[:], in_=x_grouped[:])
-        quantise_chunk("c0")
-        nc.vector.tensor_copy(out=gain[:], in_=gain_ps[:])
-        multiply_c(0)
-        regroup_vector("c1")
         regroup_scalar("c1")
+        nc.vector.quantize_mx(out=x_q[:].bitcast(FP8X4), scales=x_s[:], in_=x_grouped[:])
+        regroup_vector("c1")
+        quantise_chunk("c0")
+        multiply_c(0)
+        nc.scalar.copy(out=gain[:], in_=gain_ps[:])
         quantise_chunk("c1")
         multiply_c(1)
 
@@ -209,6 +208,7 @@ def tile_mla_pa_s_kernel(
         apply_gain(0)
         sum_squares(1)
         regroup_vector("k0")
+        regroup_vector("k1")
         quantise_chunk("k0")
         rstd = keep.tile([P, 1], F32)
         nc.scalar.activation(
@@ -221,8 +221,6 @@ def tile_mla_pa_s_kernel(
         rstd_ps = psum.tile([P, P], F32, name="bank_gain")
         nc.tensor.transpose(rstd_ps[:], rstd[:].to_broadcast([P, P]), ident[:])
         apply_gain(1)
-        regroup_scalar("k0")
-        regroup_vector("k1")
         regroup_scalar("k1")
         latent = keep.tile([P, P, PACK], BF16, align_bytes=64)
         nc.vector.tensor_tensor(
@@ -261,7 +259,7 @@ def tile_mla_pa_s_kernel(
         cross = {}
         pairs = "r (h i e) -> r h i e"
 
-        def rotation_products(h, k_ps):
+        def rotation_products(h, k_ps, pieces):
             k_pairs = k_ps[:].rearrange(pairs, i=PAIRS, e=2)
             rot[h] = keep.tile([P, CHUNK], F32, name="rot%d" % h)
             cross[h] = keep.tile([P, CHUNK], F32, name="cross%d" % h)
@@ -272,12 +270,15 @@ def tile_mla_pa_s_kernel(
                 in1=cos_sb[:].unsqueeze(1).unsqueeze(3).to_broadcast(shape),
                 op=ALU.mult,
             )
-            nc.vector.tensor_tensor(
-                out=cross[h][:].rearrange(pairs, i=PAIRS, e=2),
-                in0=k_pairs[:, :, :, ::-1],
-                in1=signed_sin[:].unsqueeze(1).to_broadcast(shape),
-                op=ALU.mult,
-            )
+            heads = CHUNK_HEADS // pieces
+            for i in range(pieces):
+                part_heads = slice(i * heads, (i + 1) * heads)
+                nc.vector.tensor_tensor(
+                    out=cross[h][:].rearrange(pairs, i=PAIRS, e=2)[:, part_heads],
+                    in0=k_pairs[:, part_heads, :, ::-1],
+                    in1=signed_sin[:].unsqueeze(1).to_broadcast([P, heads, PAIRS, 2]),
+                    op=ALU.mult,
+                )
 
         def rotation_sum(engine, h, first, width):
             cols = slice(first, first + width)
@@ -298,7 +299,7 @@ def tile_mla_pa_s_kernel(
         regroup_scalar("v0")
         regroup_scalar("v1")
         regroup_vector("v0")
-        rotation_products(0, k0_ps)
+        rotation_products(0, k0_ps, 1)
         rotation_sum(nc.gpsimd, 0, 0, CHUNK)
         regroup_vector("v1")
         quantise_chunk("v0")
@@ -307,6 +308,6 @@ def tile_mla_pa_s_kernel(
         v1_ps = multiply_chunk("v1", "bank_tok1")
         store_v(0, v0_ps)
         store_v(1, v1_ps)
-        rotation_products(1, k1_ps)
+        rotation_products(1, k1_ps, 2)
         rotation_sum(nc.vector, 1, 0, CHUNK // 2)
         rotation_sum(nc.vector, 1, CHUNK // 2, CHUNK // 2)

@@ -26,7 +26,7 @@ C_CHUNK = RANK // 2
 RUN = 4
 EPS = 1e-6
 
-VECTOR_COLS = {"c0": 256, "c1": 64, "k0": 512, "k1": 256, "v0": 64, "v1": 0}
+VECTOR_COLS = {"c0": 256, "c1": 64, "k0": 312, "k1": 128, "v0": 64, "v1": 64}
 GPSIMD_COLS = {"v0": 128, "v1": 192}
 GPSIMD_PIECES = 2
 
@@ -141,6 +141,20 @@ def tile_mla_pa_s_kernel(
         unit = keep.tile([P, PACK], BF16)
         nc.vector.tensor_copy(out=unit[:], in_=ident[:, 0:PACK])
 
+        warm_ps = psum.tile([P, CHUNK], F32, name="bank_k1")
+
+        def keep_warm_plain(count):
+            for i in range(count):
+                nc.tensor.matmul(
+                    warm_ps[:, 0:P], lhsT=ident[:], rhs=ident[:], start=True, stop=True
+                )
+
+        def keep_warm_mx(count):
+            for i in range(count):
+                matmul(warm_ps[:, 0:C_CHUNK], x_mx, (words["c0"][:], scales["c0"][:]))
+
+        keep_warm_plain(3)
+
         x_words = x_sb[:].bitcast(F32).rearrange("r (p u) -> r u p", u=2)
         xT_ps = psum.tile([P, 2, P], F32, name="bank_x")
         for u in range(2):
@@ -157,13 +171,18 @@ def tile_mla_pa_s_kernel(
         x_s = keep.tile([P, P], U8, align_bytes=64)
         x_mx = (x_q[:], x_s[:])
 
+        keep_warm_plain(2)
+
         c_tok = []
         c_chan = []
 
-        def multiply_c(h):
+        def multiply_c_tok(h):
             name = "c%d" % h
             c_tok.append(psum.tile([P, C_CHUNK], F32, name="bank_tok%d" % h))
             matmul(c_tok[h][:], x_mx, (words[name][:], scales[name][:]))
+
+        def multiply_c_chan(h):
+            name = "c%d" % h
             c_chan.append(psum.tile([P, 2, P], F32, name="bank_chan%d" % h))
             for u in range(2):
                 cols = slice(u * P, (u + 1) * P)
@@ -174,10 +193,15 @@ def tile_mla_pa_s_kernel(
         nc.vector.quantize_mx(out=x_q[:].bitcast(FP8X4), scales=x_s[:], in_=x_grouped[:])
         regroup_vector("c1")
         quantise_chunk("c0")
-        multiply_c(0)
+        multiply_c_tok(0)
         nc.scalar.copy(out=gain[:], in_=gain_ps[:])
         quantise_chunk("c1")
-        multiply_c(1)
+        multiply_c_tok(1)
+        for h in range(2):
+            multiply_c_chan(h)
+        keep_warm_mx(1)
+        regroup_vector("k0")
+        regroup_scalar("k0")
 
         sums = []
 
@@ -190,25 +214,12 @@ def tile_mla_pa_s_kernel(
 
         c_gain = keep.tile([P, PACK, P], F32)
 
-        def apply_gain(h):
-            for u in range(2):
-                t = 2 * h + u
-                nc.scalar.activation(
-                    out=c_gain[:, t, :],
-                    in_=c_chan[h][:, u, :],
-                    func=ACT.Copy,
-                    scale=gain[:, t : t + 1],
-                )
-
         sum_squares(0)
         part = keep.tile([P, 1], F32)
         nc.gpsimd.tensor_scalar(
             out=part[:], in0=sums[0][:], scalar1=1.0 / RANK, scalar2=EPS, op0=ALU.mult, op1=ALU.add
         )
-        apply_gain(0)
         sum_squares(1)
-        regroup_vector("k0")
-        regroup_vector("k1")
         quantise_chunk("k0")
         rstd = keep.tile([P, 1], F32)
         nc.scalar.activation(
@@ -220,7 +231,21 @@ def tile_mla_pa_s_kernel(
         )
         rstd_ps = psum.tile([P, P], F32, name="bank_gain")
         nc.tensor.transpose(rstd_ps[:], rstd[:].to_broadcast([P, P]), ident[:])
-        apply_gain(1)
+        keep_warm_mx(4)
+        for t in range(2):
+            nc.scalar.activation(
+                out=c_gain[:, t, :],
+                in_=c_chan[0][:, t, :],
+                func=ACT.Copy,
+                scale=gain[:, t : t + 1],
+            )
+        nc.vector.tensor_tensor(
+            out=c_gain[:, 2:4, :],
+            in0=c_chan[1][:],
+            in1=gain[:, 2:4].unsqueeze(2).to_broadcast([P, 2, P]),
+            op=ALU.mult,
+        )
+        regroup_vector("k1")
         regroup_scalar("k1")
         latent = keep.tile([P, P, PACK], BF16, align_bytes=64)
         nc.vector.tensor_tensor(
@@ -229,6 +254,7 @@ def tile_mla_pa_s_kernel(
             in1=rstd_ps[:].unsqueeze(2).to_broadcast([P, P, PACK]),
             op=ALU.mult,
         )
+        regroup_vector("v0")
         latent_q = keep.tile([P, P], U32, align_bytes=64)
         latent_s = keep.tile([P, P], U8, align_bytes=64)
         nc.vector.quantize_mx(
@@ -259,23 +285,26 @@ def tile_mla_pa_s_kernel(
         cross = {}
         pairs = "r (h i e) -> r h i e"
 
-        def rotation_products(h, k_ps, pieces):
-            k_pairs = k_ps[:].rearrange(pairs, i=PAIRS, e=2)
+        def rotation_cos(h, k_ps):
             rot[h] = keep.tile([P, CHUNK], F32, name="rot%d" % h)
             cross[h] = keep.tile([P, CHUNK], F32, name="cross%d" % h)
-            shape = [P, CHUNK_HEADS, PAIRS, 2]
             nc.vector.tensor_tensor(
                 out=rot[h][:].rearrange(pairs, i=PAIRS, e=2),
-                in0=k_pairs,
-                in1=cos_sb[:].unsqueeze(1).unsqueeze(3).to_broadcast(shape),
+                in0=k_ps[:].rearrange(pairs, i=PAIRS, e=2),
+                in1=cos_sb[:]
+                .unsqueeze(1)
+                .unsqueeze(3)
+                .to_broadcast([P, CHUNK_HEADS, PAIRS, 2]),
                 op=ALU.mult,
             )
+
+        def rotation_sin(h, k_ps, pieces):
             heads = CHUNK_HEADS // pieces
             for i in range(pieces):
                 part_heads = slice(i * heads, (i + 1) * heads)
                 nc.vector.tensor_tensor(
                     out=cross[h][:].rearrange(pairs, i=PAIRS, e=2)[:, part_heads],
-                    in0=k_pairs[:, part_heads, :, ::-1],
+                    in0=k_ps[:].rearrange(pairs, i=PAIRS, e=2)[:, part_heads, :, ::-1],
                     in1=signed_sin[:].unsqueeze(1).to_broadcast([P, heads, PAIRS, 2]),
                     op=ALU.mult,
                 )
@@ -298,16 +327,17 @@ def tile_mla_pa_s_kernel(
         k1_ps = multiply_chunk("k1", "bank_k1")
         regroup_scalar("v0")
         regroup_scalar("v1")
-        regroup_vector("v0")
-        rotation_products(0, k0_ps, 1)
-        rotation_sum(nc.gpsimd, 0, 0, CHUNK)
         regroup_vector("v1")
+        rotation_cos(0, k0_ps)
+        rotation_sin(0, k0_ps, 1)
+        rotation_sum(nc.gpsimd, 0, 0, CHUNK)
         quantise_chunk("v0")
         v0_ps = multiply_chunk("v0", "bank_tok0")
+        rotation_cos(1, k1_ps)
         quantise_chunk("v1")
         v1_ps = multiply_chunk("v1", "bank_tok1")
         store_v(0, v0_ps)
-        store_v(1, v1_ps)
-        rotation_products(1, k1_ps, 2)
+        rotation_sin(1, k1_ps, 2)
         rotation_sum(nc.vector, 1, 0, CHUNK // 2)
+        store_v(1, v1_ps)
         rotation_sum(nc.vector, 1, CHUNK // 2, CHUNK // 2)

@@ -26,7 +26,7 @@ C_CHUNK = RANK // 2
 RUN = 4
 EPS = 1e-6
 
-VECTOR_COLS = {"c0": 256, "c1": 64, "k0": 312, "k1": 128, "v0": 64, "v1": 64}
+VECTOR_COLS = {"c0": 256, "c1": 64, "k0": 512, "k1": 144, "v0": 112, "v1": 0}
 GPSIMD_COLS = {"v0": 128, "v1": 192}
 GPSIMD_PIECES = 2
 
@@ -123,12 +123,12 @@ def tile_mla_pa_s_kernel(
             out=gain_rows[0:PACK, :], in_=kv_norm_w.rearrange("(t p) -> t p", t=PACK)
         )
         load(["k0"], k_view, 0, CHUNK)
+        load(["k1"], k_view, CHUNK, CHUNK)
         cos_sb = keep.tile([P, PAIRS], BF16)
         sin_sb = keep.tile([P, PAIRS], BF16)
         for b in range(BATCH):
             nc.sync.dma_start(out=cos_sb[b * SEQ : (b + 1) * SEQ, :], in_=freqs_cos)
             nc.sync.dma_start(out=sin_sb[b * SEQ : (b + 1) * SEQ, :], in_=freqs_sin)
-        load(["k1"], k_view, CHUNK, CHUNK)
         for h in range(2):
             load(["v%d" % h], v_view, h * CHUNK, CHUNK)
 
@@ -140,20 +140,6 @@ def tile_mla_pa_s_kernel(
         nc.scalar.activation(out=warm[:], in_=one[:], func=ACT.Abs_reciprocal_sqrt)
         unit = keep.tile([P, PACK], BF16)
         nc.vector.tensor_copy(out=unit[:], in_=ident[:, 0:PACK])
-
-        warm_ps = psum.tile([P, CHUNK], F32, name="bank_k1")
-
-        def keep_warm_plain(count):
-            for i in range(count):
-                nc.tensor.matmul(
-                    warm_ps[:, 0:P], lhsT=ident[:], rhs=ident[:], start=True, stop=True
-                )
-
-        def keep_warm_mx(count):
-            for i in range(count):
-                matmul(warm_ps[:, 0:C_CHUNK], x_mx, (words["c0"][:], scales["c0"][:]))
-
-        keep_warm_plain(3)
 
         x_words = x_sb[:].bitcast(F32).rearrange("r (p u) -> r u p", u=2)
         xT_ps = psum.tile([P, 2, P], F32, name="bank_x")
@@ -170,8 +156,6 @@ def tile_mla_pa_s_kernel(
         x_q = keep.tile([P, P], U32, align_bytes=64)
         x_s = keep.tile([P, P], U8, align_bytes=64)
         x_mx = (x_q[:], x_s[:])
-
-        keep_warm_plain(2)
 
         c_tok = []
         c_chan = []
@@ -199,7 +183,6 @@ def tile_mla_pa_s_kernel(
         multiply_c_tok(1)
         for h in range(2):
             multiply_c_chan(h)
-        keep_warm_mx(1)
         regroup_vector("k0")
         regroup_scalar("k0")
 
@@ -231,21 +214,13 @@ def tile_mla_pa_s_kernel(
         )
         rstd_ps = psum.tile([P, P], F32, name="bank_gain")
         nc.tensor.transpose(rstd_ps[:], rstd[:].to_broadcast([P, P]), ident[:])
-        keep_warm_mx(4)
-        for t in range(2):
+        for t in range(PACK):
             nc.scalar.activation(
                 out=c_gain[:, t, :],
-                in_=c_chan[0][:, t, :],
+                in_=c_chan[t // 2][:, t % 2, :],
                 func=ACT.Copy,
                 scale=gain[:, t : t + 1],
             )
-        nc.vector.tensor_tensor(
-            out=c_gain[:, 2:4, :],
-            in0=c_chan[1][:],
-            in1=gain[:, 2:4].unsqueeze(2).to_broadcast([P, 2, P]),
-            op=ALU.mult,
-        )
-        regroup_vector("k1")
         regroup_scalar("k1")
         latent = keep.tile([P, P, PACK], BF16, align_bytes=64)
         nc.vector.tensor_tensor(
@@ -254,7 +229,7 @@ def tile_mla_pa_s_kernel(
             in1=rstd_ps[:].unsqueeze(2).to_broadcast([P, P, PACK]),
             op=ALU.mult,
         )
-        regroup_vector("v0")
+        regroup_vector("k1")
         latent_q = keep.tile([P, P], U32, align_bytes=64)
         latent_s = keep.tile([P, P], U8, align_bytes=64)
         nc.vector.quantize_mx(
@@ -327,17 +302,17 @@ def tile_mla_pa_s_kernel(
         k1_ps = multiply_chunk("k1", "bank_k1")
         regroup_scalar("v0")
         regroup_scalar("v1")
-        regroup_vector("v1")
+        regroup_vector("v0")
         rotation_cos(0, k0_ps)
         rotation_sin(0, k0_ps, 1)
         rotation_sum(nc.gpsimd, 0, 0, CHUNK)
         quantise_chunk("v0")
         v0_ps = multiply_chunk("v0", "bank_tok0")
-        rotation_cos(1, k1_ps)
         quantise_chunk("v1")
         v1_ps = multiply_chunk("v1", "bank_tok1")
         store_v(0, v0_ps)
+        store_v(1, v1_ps)
+        rotation_cos(1, k1_ps)
         rotation_sin(1, k1_ps, 2)
         rotation_sum(nc.vector, 1, 0, CHUNK // 2)
-        store_v(1, v1_ps)
         rotation_sum(nc.vector, 1, CHUNK // 2, CHUNK // 2)

@@ -304,13 +304,13 @@ def tile_mla_pa_s_kernel(
         regroup_scalar("v1")
         regroup_vector("v0")
         rotation_cos(0, k0_ps)
-        rotation_sin(0, k0_ps, 1)
-        rotation_sum(nc.gpsimd, 0, 0, CHUNK)
         quantise_chunk("v0")
         v0_ps = multiply_chunk("v0", "bank_tok0")
+        store_v(0, v0_ps)
+        rotation_sin(0, k0_ps, 1)
+        rotation_sum(nc.gpsimd, 0, 0, CHUNK)
         quantise_chunk("v1")
         v1_ps = multiply_chunk("v1", "bank_tok1")
-        store_v(0, v0_ps)
         store_v(1, v1_ps)
         rotation_cos(1, k1_ps)
         rotation_sin(1, k1_ps, 2)

@@ -26,8 +26,8 @@ C_CHUNK = RANK // 2
 RUN = 4
 EPS = 1e-6
 
-VECTOR_COLS = {"c0": 256, "c1": 64, "k0": 512, "k1": 144, "v0": 112, "v1": 0}
-GPSIMD_COLS = {"v0": 128, "v1": 192}
+VECTOR_COLS = {"c0": 256, "c1": 64, "k0": 384, "k1": 224, "v0": 160, "v1": 0}
+GPSIMD_COLS = {"v0": 96, "v1": 144}
 GPSIMD_PIECES = 2
 
 FLOPS = 2 * P * D_MODEL * RANK + 2 * 2 * P * RANK * HEADS * HEAD_DIM
@@ -72,9 +72,9 @@ def tile_mla_pa_s_kernel(
                 in_=raw[name][:, :, cols].rearrange("p t (c i) -> p c t i", i=RUN),
             )
 
-        def regroup_vector(name):
-            if VECTOR_COLS[name] > 0:
-                regroup(nc.vector.tensor_copy, name, slice(0, VECTOR_COLS[name]))
+        def regroup_vector(name, part=0, parts=1):
+            width = VECTOR_COLS[name] // parts
+            regroup(nc.vector.tensor_copy, name, slice(part * width, (part + 1) * width))
 
         def copy_gpsimd(out, in_):
             nc.gpsimd.tensor_scalar(
@@ -204,6 +204,7 @@ def tile_mla_pa_s_kernel(
         )
         sum_squares(1)
         quantise_chunk("k0")
+        regroup_vector("k1", 0, 2)
         rstd = keep.tile([P, 1], F32)
         nc.scalar.activation(
             out=rstd[:],
@@ -229,7 +230,7 @@ def tile_mla_pa_s_kernel(
             in1=rstd_ps[:].unsqueeze(2).to_broadcast([P, P, PACK]),
             op=ALU.mult,
         )
-        regroup_vector("k1")
+        regroup_vector("k1", 1, 2)
         latent_q = keep.tile([P, P], U32, align_bytes=64)
         latent_s = keep.tile([P, P], U8, align_bytes=64)
         nc.vector.quantize_mx(
@@ -298,11 +299,11 @@ def tile_mla_pa_s_kernel(
             nc.sync.dma_start(out=v_rows[:, h * CHUNK : (h + 1) * CHUNK], in_=v_sb[:])
 
         k0_ps = multiply_chunk("k0", "bank_k0")
+        regroup_vector("v0")
         quantise_chunk("k1")
         k1_ps = multiply_chunk("k1", "bank_k1")
         regroup_scalar("v0")
         regroup_scalar("v1")
-        regroup_vector("v0")
         rotation_cos(0, k0_ps)
         quantise_chunk("v0")
         v0_ps = multiply_chunk("v0", "bank_tok0")

from contextlib import ExitStack

import concourse.mybir as mybir
from concourse.masks import make_identity

F32 = mybir.dt.float32
BF16 = mybir.dt.bfloat16
U32 = mybir.dt.uint32
U8 = mybir.dt.uint8
FP8X4 = mybir.dt.float8_e4m3fn_x4
ACT = mybir.ActivationFunctionType
ALU = mybir.AluOpType

P = 128
PACK = 4
BATCH = 2
SEQ = 64
D_MODEL = 512
RANK = 512
HEADS = 16
HEAD_DIM = 64
PAIRS = HEAD_DIM // 2
CHUNK = 512
CHUNK_HEADS = CHUNK // HEAD_DIM
C_CHUNK = RANK // 2
RUN = 4
EPS = 1e-6

VECTOR_COLS = {"c0": 256, "c1": 64, "k0": 384, "k1": 224, "v0": 160, "v1": 0}
GPSIMD_COLS = {"v0": 96, "v1": 144}
GPSIMD_PIECES = 2

FLOPS = 2 * P * D_MODEL * RANK + 2 * 2 * P * RANK * HEADS * HEAD_DIM


def tile_mla_pa_s_kernel(
    tc, x, freqs_cos, freqs_sin, w_kv_compress, kv_norm_w, w_k_up, w_v_up, out_0, out_1
):
    nc = tc.nc
    x_rows = x.rearrange("b s d -> (b s) d")
    k_rows = out_0.rearrange("b s h d -> (b s) (h d)")
    v_rows = out_1.rearrange("b s h d -> (b s) (h d)")

    with ExitStack() as ctx:
        keep = ctx.enter_context(tc.tile_pool(name="keep", bufs=1))
        psum = ctx.enter_context(tc.psum_pool(name="psum", bufs=1))
        ctx.enter_context(tc.manual_schedule())

        raw = {}
        grouped = {}
        words = {}
        scales = {}

        def load(names, view, first_col, width):
            cols = len(names) * width
            tile = keep.tile([P, PACK, cols], BF16, name="raw_%s" % names[0])
            nc.sync.dma_start(out=tile[:], in_=view[:, :, first_col : first_col + cols])
            for i, name in enumerate(names):
                make_chunk(name, tile[:, :, i * width : (i + 1) * width], width)

        def make_chunk(name, raw_cols, width):
            raw[name] = raw_cols
            grouped[name] = keep.tile(
                [P, width, PACK], BF16, name="grouped_%s" % name, align_bytes=64
            )
            words[name] = keep.tile([P, width], U32, name="words_%s" % name, align_bytes=64)
            scales[name] = keep.tile([P, width], U8, name="scales_%s" % name, align_bytes=64)

        def regroup(copy, name, cols):
            copy(
                out=grouped[name][:, cols, :].rearrange("p (c i) t -> p c t i", i=RUN),
                in_=raw[name][:, :, cols].rearrange("p t (c i) -> p c t i", i=RUN),
            )

        def regroup_vector(name, part=0, parts=1):
            width = VECTOR_COLS[name] // parts
            regroup(nc.vector.tensor_copy, name, slice(part * width, (part + 1) * width))

        def copy_gpsimd(out, in_):
            nc.gpsimd.tensor_scalar(
                out=out, in0=in_, scalar1=1.0, scalar2=0.0, op0=ALU.mult, op1=ALU.add
            )

        def regroup_gpsimd(name):
            piece = GPSIMD_COLS[name] // GPSIMD_PIECES
            for i in range(GPSIMD_PIECES):
                first = VECTOR_COLS[name] + i * piece
                regroup(copy_gpsimd, name, slice(first, first + piece))

        def regroup_scalar(name):
            width = raw[name].shape[2]
            first = VECTOR_COLS[name] + GPSIMD_COLS.get(name, 0)
            if first < width:
                regroup(nc.scalar.copy, name, slice(first, width))

        def quantise_chunk(name):
            nc.vector.quantize_mx(
                out=words[name][:].bitcast(FP8X4),
                scales=scales[name][:],
                in_=grouped[name][:].rearrange("p c t -> p (c t)"),
            )

        def matmul(out, lhsT, rhs):
            nc.tensor.matmul_mx(
                out=out,
                lhsT=lhsT[0].bitcast(FP8X4),
                lhsT_scale=lhsT[1],
                rhs=rhs[0].bitcast(FP8X4),
                rhs_scale=rhs[1],
                start=True,
                stop=True,
            )

        x_sb = keep.tile([P, D_MODEL], BF16)
        nc.sync.dma_start(out=x_sb[:], in_=x_rows)
        c_view = w_kv_compress.rearrange("(p t) c -> p t c", t=PACK)
        k_view = w_k_up.rearrange("(t p) c -> p t c", t=PACK)
        v_view = w_v_up.rearrange("(t p) c -> p t c", t=PACK)
        load(["c0", "c1"], c_view, 0, C_CHUNK)
        gain_rows = keep.tile([P, P], BF16)
        nc.vector.memset(gain_rows[:], 0.0)
        nc.sync.dma_start(
            out=gain_rows[0:PACK, :], in_=kv_norm_w.rearrange("(t p) -> t p", t=PACK)
        )
        load(["k0"], k_view, 0, CHUNK)
        load(["k1"], k_view, CHUNK, CHUNK)
        cos_sb = keep.tile([P, PAIRS], BF16)
        sin_sb = keep.tile([P, PAIRS], BF16)
        for b in range(BATCH):
            nc.sync.dma_start(out=cos_sb[b * SEQ : (b + 1) * SEQ, :], in_=freqs_cos)
            nc.sync.dma_start(out=sin_sb[b * SEQ : (b + 1) * SEQ, :], in_=freqs_sin)
        for h in range(2):
            load(["v%d" % h], v_view, h * CHUNK, CHUNK)

        ident = keep.tile([P, P], F32)
        make_identity(nc, ident[:])
        one = keep.tile([P, 1], F32)
        nc.vector.memset(one[:], 1.0)
        warm = keep.tile([P, 1], F32)
        nc.scalar.activation(out=warm[:], in_=one[:], func=ACT.Abs_reciprocal_sqrt)
        unit = keep.tile([P, PACK], BF16)
        nc.vector.tensor_copy(out=unit[:], in_=ident[:, 0:PACK])

        x_words = x_sb[:].bitcast(F32).rearrange("r (p u) -> r u p", u=2)
        xT_ps = psum.tile([P, 2, P], F32, name="bank_x")
        for u in range(2):
            nc.tensor.transpose(xT_ps[:, u, :], x_words[:, u, :], ident[:])
        gain_ps = psum.tile([P, PACK], F32, name="bank_gain")
        nc.tensor.matmul(gain_ps[:], lhsT=gain_rows[:], rhs=unit[:], start=True, stop=True)
        gain = keep.tile([P, PACK], F32)
        x_grouped = keep.tile([P, P * PACK], BF16, align_bytes=64)
        nc.vector.tensor_copy(
            out=x_grouped[:].bitcast(F32).rearrange("p (r u) -> p r u", u=2),
            in_=xT_ps[:].rearrange("p u r -> p r u"),
        )
        x_q = keep.tile([P, P], U32, align_bytes=64)
        x_s = keep.tile([P, P], U8, align_bytes=64)
        x_mx = (x_q[:], x_s[:])

        c_tok = []
        c_chan = []

        def multiply_c_tok(h):
            name = "c%d" % h
            c_tok.append(psum.tile([P, C_CHUNK], F32, name="bank_tok%d" % h))
            matmul(c_tok[h][:], x_mx, (words[name][:], scales[name][:]))

        def multiply_c_chan(h):
            name = "c%d" % h
            c_chan.append(psum.tile([P, 2, P], F32, name="bank_chan%d" % h))
            for u in range(2):
                cols = slice(u * P, (u + 1) * P)
                matmul(c_chan[h][:, u, :], (words[name][:, cols], scales[name][:, cols]), x_mx)

        regroup_vector("c0")
        regroup_scalar("c1")
        nc.vector.quantize_mx(out=x_q[:].bitcast(FP8X4), scales=x_s[:], in_=x_grouped[:])
        regroup_vector("c1")
        quantise_chunk("c0")
        multiply_c_tok(0)
        nc.scalar.copy(out=gain[:], in_=gain_ps[:])
        quantise_chunk("c1")
        multiply_c_tok(1)
        for h in range(2):
            multiply_c_chan(h)
        regroup_vector("k0")
        regroup_scalar("k0")

        sums = []

        def sum_squares(h):
            squares = keep.tile([P, C_CHUNK], BF16, name="squares%d" % h)
            sums.append(keep.tile([P, 1], F32, name="sum%d" % h))
            nc.scalar.activation(
                out=squares[:], in_=c_tok[h][:], func=ACT.Square, accum_out=sums[h][:]
            )

        c_gain = keep.tile([P, PACK, P], F32)

        sum_squares(0)
        part = keep.tile([P, 1], F32)
        nc.gpsimd.tensor_scalar(
            out=part[:], in0=sums[0][:], scalar1=1.0 / RANK, scalar2=EPS, op0=ALU.mult, op1=ALU.add
        )
        sum_squares(1)
        quantise_chunk("k0")
        regroup_vector("k1", 0, 2)
        rstd = keep.tile([P, 1], F32)
        nc.scalar.activation(
            out=rstd[:],
            in_=sums[1][:],
            func=ACT.Abs_reciprocal_sqrt,
            scale=1.0 / RANK,
            bias=part[:],
        )
        rstd_ps = psum.tile([P, P], F32, name="bank_gain")
        nc.tensor.transpose(rstd_ps[:], rstd[:].to_broadcast([P, P]), ident[:])
        for t in range(PACK):
            nc.scalar.activation(
                out=c_gain[:, t, :],
                in_=c_chan[t // 2][:, t % 2, :],
                func=ACT.Copy,
                scale=gain[:, t : t + 1],
            )
        regroup_scalar("k1")
        latent = keep.tile([P, P, PACK], BF16, align_bytes=64)
        nc.vector.tensor_tensor(
            out=latent[:],
            in0=c_gain[:].rearrange("p t r -> p r t"),
            in1=rstd_ps[:].unsqueeze(2).to_broadcast([P, P, PACK]),
            op=ALU.mult,
        )
        regroup_vector("k1", 1, 2)
        latent_q = keep.tile([P, P], U32, align_bytes=64)
        latent_s = keep.tile([P, P], U8, align_bytes=64)
        nc.vector.quantize_mx(
            out=latent_q[:].bitcast(FP8X4),
            scales=latent_s[:],
            in_=latent[:].rearrange("p r t -> p (r t)"),
        )
        latent_mx = (latent_q[:], latent_s[:])

        def multiply_chunk(name, bank):
            acc = psum.tile([P, CHUNK], F32, name=bank)
            matmul(acc[:], latent_mx, (words[name][:], scales[name][:]))
            return acc

        signed_sin = keep.tile([P, PAIRS, 2], F32)
        for e in range(2):
            nc.gpsimd.tensor_scalar(
                out=signed_sin[:, :, e],
                in0=sin_sb[:],
                scalar1=2.0 * e - 1.0,
                scalar2=0.0,
                op0=ALU.mult,
                op1=ALU.add,
            )
        regroup_gpsimd("v0")
        regroup_gpsimd("v1")
        rot = {}
        cross = {}
        pairs = "r (h i e) -> r h i e"

        def rotation_cos(h, k_ps):
            rot[h] = keep.tile([P, CHUNK], F32, name="rot%d" % h)
            cross[h] = keep.tile([P, CHUNK], F32, name="cross%d" % h)
            nc.vector.tensor_tensor(
                out=rot[h][:].rearrange(pairs, i=PAIRS, e=2),
                in0=k_ps[:].rearrange(pairs, i=PAIRS, e=2),
                in1=cos_sb[:]
                .unsqueeze(1)
                .unsqueeze(3)
                .to_broadcast([P, CHUNK_HEADS, PAIRS, 2]),
                op=ALU.mult,
            )

        def rotation_sin(h, k_ps, pieces):
            heads = CHUNK_HEADS // pieces
            for i in range(pieces):
                part_heads = slice(i * heads, (i + 1) * heads)
                nc.vector.tensor_tensor(
                    out=cross[h][:].rearrange(pairs, i=PAIRS, e=2)[:, part_heads],
                    in0=k_ps[:].rearrange(pairs, i=PAIRS, e=2)[:, part_heads, :, ::-1],
                    in1=signed_sin[:].unsqueeze(1).to_broadcast([P, heads, PAIRS, 2]),
                    op=ALU.mult,
                )

        def rotation_sum(engine, h, first, width):
            cols = slice(first, first + width)
            engine.tensor_tensor(
                out=rot[h][:, cols], in0=rot[h][:, cols], in1=cross[h][:, cols], op=ALU.add
            )
            out_cols = slice(h * CHUNK + first, h * CHUNK + first + width)
            nc.sync.dma_start(out=k_rows[:, out_cols], in_=rot[h][:, cols])

        def store_v(h, acc):
            v_sb = keep.tile([P, CHUNK], F32, name="v_sb%d" % h)
            nc.scalar.copy(out=v_sb[:], in_=acc[:])
            nc.sync.dma_start(out=v_rows[:, h * CHUNK : (h + 1) * CHUNK], in_=v_sb[:])

        k0_ps = multiply_chunk("k0", "bank_k0")
        regroup_vector("v0")
        quantise_chunk("k1")
        k1_ps = multiply_chunk("k1", "bank_k1")
        regroup_scalar("v0")
        regroup_scalar("v1")
        rotation_cos(0, k0_ps)
        quantise_chunk("v0")
        v0_ps = multiply_chunk("v0", "bank_tok0")
        store_v(0, v0_ps)
        rotation_sin(0, k0_ps, 1)
        rotation_sum(nc.gpsimd, 0, 0, CHUNK)
        quantise_chunk("v1")
        v1_ps = multiply_chunk("v1", "bank_tok1")
        store_v(1, v1_ps)
        rotation_cos(1, k1_ps)
        rotation_sin(1, k1_ps, 2)
        rotation_sum(nc.vector, 1, 0, CHUNK // 2)
        rotation_sum(nc.vector, 1, CHUNK // 2, CHUNK // 2)
